import numpy as np
import ml_dtypes


def mxq(x, axis, fmt="e4m3"):
    dtype, down = {"e4m3": (ml_dtypes.float8_e4m3fn, 7), "e5m2": (ml_dtypes.float8_e5m2, 14)}[fmt]
    v = np.moveaxis(np.asarray(x, np.float32).astype(ml_dtypes.bfloat16).astype(np.float64), axis, -1)
    blocks = v.reshape(v.shape[:-1] + (-1, 32))
    amax = np.abs(blocks).max(-1, keepdims=True)
    byte = np.maximum(np.where(amax > 0, np.frexp(amax)[1] - 1 + 127, 0) - down, 1)
    scale = np.exp2(byte - 127.0)
    codes = (blocks / scale).astype(np.float32).astype(dtype).astype(np.float64)
    return np.moveaxis((codes * scale).reshape(v.shape), -1, axis)


BF16 = ml_dtypes.bfloat16


def bf(x):
    return np.asarray(x, np.float32).astype(BF16)


def f64(x):
    return np.asarray(x).astype(np.float64)


B, N, F = 32, 256, 512

EMP = 0.1
EPS = 1e-8
ZERO = 9e-15


def setup_inputs():
    g = np.random.standard_normal((B, 1, F))
    a = (1.0 + 2.0 * np.random.random((B, N, 1))) * (2.0 * np.random.randint(0, 2, (B, N, 1)) - 1.0)
    x = np.random.standard_normal((B, N, F)) + a * g
    w = 1.0 + 0.5 * np.random.standard_normal((1, N, F))
    return {"x": bf(x), "w": bf(w)}


def reference(x, w):
    xw = f64(x) * f64(w)
    nrm = np.maximum(np.sqrt(np.sum(xw * xw, axis=-1, keepdims=True)), EPS)
    xn = xw / nrm
    xq = mxq(xn, 2, "e4m3")
    cos = xq @ xq.transpose(0, 2, 1)
    return np.where(cos > EMP, cos, ZERO)

@@ -1,0 +1,217 @@
+from contextlib import ExitStack
+
+import concourse.mybir as mybir
+from concourse.masks import make_identity
+
+FLOPS = 2 * 32 * 256 * 256 * 512
+
+F32 = mybir.dt.float32
+BF16 = mybir.dt.bfloat16
+U32 = mybir.dt.uint32
+U8 = mybir.dt.uint8
+FP8X4 = mybir.dt.float8_e4m3fn_x4
+ALU = mybir.AluOpType
+ACT = mybir.ActivationFunctionType
+
+P = 128
+EMP = 0.1
+EPS = 1e-8
+ZERO = 9e-15
+
+LOAD_B = 2
+GA = 2
+STORE_B = 2
+D_CH = 1
+D_N = 2
+D_T = 4
+D_Q = 5
+MANUAL = True
+W_PSUM = True
+
+
+def tile_simmetricblock_t_kernel(tc, x, w, out):
+    nc = tc.nc
+    nb, nn, nf = x.shape
+    nh = nn // P
+    nt = nf // P
+    with ExitStack() as ctx:
+        const = ctx.enter_context(tc.tile_pool(name="const", bufs=1))
+        xin = ctx.enter_context(tc.tile_pool(name="xin", bufs=nb // LOAD_B))
+        xwp = ctx.enter_context(tc.tile_pool(name="xwp", bufs=8))
+        junkp = ctx.enter_context(tc.tile_pool(name="junkp", bufs=2))
+        xnp = ctx.enter_context(tc.tile_pool(name="xnp", bufs=4))
+        grp = ctx.enter_context(tc.tile_pool(name="grp", bufs=3))
+        mxp = ctx.enter_context(tc.tile_pool(name="mxp", bufs=3))
+        qp = ctx.enter_context(tc.tile_pool(name="qp", bufs=3))
+        op = ctx.enter_context(tc.tile_pool(name="op", bufs=3))
+        psw = ctx.enter_context(tc.psum_pool(name="psw", bufs=1))
+        pst = ctx.enter_context(tc.psum_pool(name="pst", bufs=3))
+        psa = ctx.enter_context(tc.psum_pool(name="psa", bufs=3))
+        if MANUAL:
+            ctx.enter_context(tc.manual_schedule())
+
+        one = const.tile([P, 1], F32)
+        nc.vector.memset(one[:], 1.0)
+        warm = const.tile([P, 1], F32)
+        nc.scalar.activation(out=warm[:], in_=one[:], func=ACT.Sqrt)
+        ident = const.tile([P, P], BF16)
+        make_identity(nc, ident[:])
+        w_sb = const.tile([P, nh, nf], BF16)
+        nc.sync.dma_start(out=w_sb[:], in_=w.rearrange("o (h p) k -> p (o h) k", p=P))
+        ss = const.tile([P, nb * nh], F32)
+        nrm = const.tile([P, nb * nh], F32)
+        nrc = const.tile([P, nb * nh], F32)
+        rinv = const.tile([P, nb * nh], F32)
+
+        x_tiles = []
+        for l in range(nb // LOAD_B):
+            x_sb = xin.tile([P, LOAD_B * nh, nf], BF16)
+            nc.sync.dma_start(
+                out=x_sb[:],
+                in_=x[l * LOAD_B : (l + 1) * LOAD_B].rearrange("b (h p) k -> p (b h) k", p=P),
+            )
+            x_tiles.append(x_sb)
+
+        if W_PSUM:
+            w_use = psw.tile([P, nh, nf], BF16)
+            for h in range(nh):
+                nc.tensor.matmul(
+                    out=w_use[:, h, :], lhsT=ident[:], rhs=w_sb[:, h, :], start=True, stop=True
+                )
+        else:
+            w_use = w_sb
+
+        xw_tiles = {}
+        xn_tiles = {}
+        xt_tiles = {}
+        gr_tiles = {}
+        o_tiles = {}
+
+        def mul_w(b):
+            x_sb = x_tiles[b // LOAD_B]
+            i = b % LOAD_B
+            xw = xwp.tile([P, nh, nf], F32)
+            xw_tiles[b] = xw
+            nc.vector.tensor_tensor(
+                out=xw[:], in0=x_sb[:, i * nh : (i + 1) * nh, :], in1=w_use[:], op=ALU.mult
+            )
+
+        def sumsq(b):
+            xw = xw_tiles[b]
+            for h in range(nh):
+                junk = junkp.tile([P, nf], BF16)
+                j = b * nh + h
+                nc.scalar.activation(
+                    out=junk[:], in_=xw[:, h, :], func=ACT.Square, accum_out=ss[:, j : j + 1]
+                )
+
+        def chain_s(g):
+            cols = slice(g * GA * nh, (g + 1) * GA * nh)
+            nc.scalar.activation(out=nrm[:, cols], in_=ss[:, cols], func=ACT.Sqrt)
+
+        def chain_v(g):
+            cols = slice(g * GA * nh, (g + 1) * GA * nh)
+            nc.vector.tensor_scalar_max(out=nrc[:, cols], in0=nrm[:, cols], scalar1=EPS)
+            nc.vector.reciprocal(out=rinv[:, cols], in_=nrc[:, cols])
+
+        def normalise(b):
+            xw = xw_tiles[b]
+            xn = xnp.tile([P, nh, nf], BF16)
+            xn_tiles[b] = xn
+            for h in range(nh):
+                j = b * nh + h
+                nc.gpsimd.tensor_scalar(
+                    out=xn[:, h, :], in0=xw[:, h, :], scalar1=rinv[:, j : j + 1],
+                    scalar2=0.0, op0=ALU.mult, op1=ALU.add,
+                )
+
+        def transposes(b):
+            xn = xn_tiles[b]
+            xt = pst.tile([P, nt, nn], BF16)
+            xt_tiles[b] = xt
+            for h in range(nh):
+                for t in range(nt):
+                    nc.tensor.transpose(
+                        xt[:, t, h * P : (h + 1) * P], xn[:, h, t * P : (t + 1) * P], ident[:]
+                    )
+
+        def copy_out(b):
+            xt = xt_tiles[b]
+            grouped = grp.tile([P, nn, nt], BF16, align_bytes=64)
+            gr_tiles[b] = grouped
+            nc.scalar.copy(out=grouped[:], in_=xt[:].rearrange("p t r -> p r t"))
+
+        mx_tiles = {}
+
+        def quantise(b):
+            grouped = gr_tiles[b]
+            codes = mxp.tile([P, nn], U32, align_bytes=64)
+            scl = mxp.tile([P, nn], U8, align_bytes=64)
+            mx_tiles[b] = (codes, scl)
+            nc.vector.quantize_mx(
+                out=codes[:].bitcast(FP8X4), scales=scl[:],
+                in_=grouped[:].rearrange("p r t -> p (r t)"),
+            )
+
+        acc_tiles = {}
+
+        def mx(b):
+            codes, scl = mx_tiles[b]
+            acc = psa.tile([P, nh, nn], F32)
+            acc_tiles[b] = acc
+            for m in range(nh):
+                nc.tensor.matmul_mx(
+                    out=acc[:, m, :],
+                    lhsT=codes[:, m * P : (m + 1) * P].bitcast(FP8X4),
+                    lhsT_scale=scl[:, m * P : (m + 1) * P],
+                    rhs=codes[:].bitcast(FP8X4),
+                    rhs_scale=scl[:],
+                    start=True,
+                    stop=True,
+                )
+
+        def threshold(b):
+            accf = acc_tiles[b][:].rearrange("p m j -> p (m j)")
+            q = qp.tile([P, nh * nn], F32)
+            nc.vector.tensor_scalar(
+                out=q[:], in0=accf, scalar1=EMP, scalar2=ZERO / EMP, op0=ALU.is_gt, op1=ALU.max
+            )
+            s = b // STORE_B
+            i = b % STORE_B
+            if i == 0:
+                o_new = op.tile([P, STORE_B, nh * nn], F32)
+                o_tiles[s] = o_new
+            o_sb = o_tiles[s]
+            nc.vector.scalar_tensor_tensor(
+                out=o_sb[:, i, :], in0=accf, scalar=EMP, in1=q[:], op0=ALU.max, op1=ALU.mult
+            )
+            if i == STORE_B - 1:
+                nc.sync.dma_start(
+                    out=out[s * STORE_B : (s + 1) * STORE_B].rearrange(
+                        "b (m p) j -> p (b m) j", p=P
+                    ),
+                    in_=o_sb[:].rearrange("p b (m j) -> p (b m) j", m=nh),
+                )
+
+        def live(b):
+            return 0 <= b < nb
+
+        for s in range(nb + D_Q + 1):
+            if live(s - D_T):
+                transposes(s - D_T)
+                copy_out(s - D_T)
+            if live(s - D_Q):
+                quantise(s - D_Q)
+                mx(s - D_Q)
+            e = s - D_CH
+            if live(e) and e % GA == GA - 1:
+                chain_s(e // GA)
+            if live(s):
+                mul_w(s)
+                sumsq(s)
+            if live(e) and e % GA == GA - 1:
+                chain_v(e // GA)
+            if live(s - D_Q):
+                threshold(s - D_Q)
+            if live(s - D_N):
+                normalise(s - D_N)

@@ -21,11 +21,17 @@ ZERO = 9e-15
 LOAD_B = 2
 GA = 2
 STORE_B = 2
-D_CH = 1
-D_N = 2
-D_T = 4
-D_Q = 5
+D_S = 1
+D_CH = 2
+D_N = 3
+D_T = 5
+D_C = 6
+D_Q = 7
+D_H = 8
 MANUAL = True
+G_MOD = 5
+G_RES = (1, 3)
+G_AHEAD = 3
 W_PSUM = True
 
 
@@ -37,7 +43,7 @@ def tile_simmetricblock_t_kernel(tc, x, w, out):
     with ExitStack() as ctx:
         const = ctx.enter_context(tc.tile_pool(name="const", bufs=1))
         xin = ctx.enter_context(tc.tile_pool(name="xin", bufs=nb // LOAD_B))
-        xwp = ctx.enter_context(tc.tile_pool(name="xwp", bufs=8))
+        xwp = ctx.enter_context(tc.tile_pool(name="xwp", bufs=14))
         junkp = ctx.enter_context(tc.tile_pool(name="junkp", bufs=2))
         xnp = ctx.enter_context(tc.tile_pool(name="xnp", bufs=4))
         grp = ctx.enter_context(tc.tile_pool(name="grp", bufs=3))
@@ -46,7 +52,7 @@ def tile_simmetricblock_t_kernel(tc, x, w, out):
         op = ctx.enter_context(tc.tile_pool(name="op", bufs=3))
         psw = ctx.enter_context(tc.psum_pool(name="psw", bufs=1))
         pst = ctx.enter_context(tc.psum_pool(name="pst", bufs=3))
-        psa = ctx.enter_context(tc.psum_pool(name="psa", bufs=3))
+        psa = ctx.enter_context(tc.psum_pool(name="psa", bufs=4))
         if MANUAL:
             ctx.enter_context(tc.manual_schedule())
 
@@ -87,10 +93,23 @@ def tile_simmetricblock_t_kernel(tc, x, w, out):
         gr_tiles = {}
         o_tiles = {}
 
+        def on_g(b):
+            return b >= G_AHEAD and b % G_MOD in G_RES
+
+        def mul_w_g(b, h):
+            x_sb = x_tiles[b // LOAD_B]
+            i = b % LOAD_B
+            if h == 0:
+                xw_new = xwp.tile([P, nh, nf], F32, name="xw")
+                xw_tiles[b] = xw_new
+            nc.gpsimd.tensor_tensor(
+                out=xw_tiles[b][:, h, :], in0=x_sb[:, i * nh + h, :], in1=w_sb[:, h, :], op=ALU.mult
+            )
+
         def mul_w(b):
             x_sb = x_tiles[b // LOAD_B]
             i = b % LOAD_B
-            xw = xwp.tile([P, nh, nf], F32)
+            xw = xwp.tile([P, nh, nf], F32, name="xw")
             xw_tiles[b] = xw
             nc.vector.tensor_tensor(
                 out=xw[:], in0=x_sb[:, i * nh : (i + 1) * nh, :], in1=w_use[:], op=ALU.mult
@@ -196,22 +215,28 @@ def tile_simmetricblock_t_kernel(tc, x, w, out):
         def live(b):
             return 0 <= b < nb
 
-        for s in range(nb + D_Q + 1):
-            if live(s - D_T):
-                transposes(s - D_T)
-                copy_out(s - D_T)
-            if live(s - D_Q):
-                quantise(s - D_Q)
-                mx(s - D_Q)
+        for s in range(nb + D_H + 1):
             e = s - D_CH
             if live(e) and e % GA == GA - 1:
                 chain_s(e // GA)
-            if live(s):
+            if live(s - D_H):
+                threshold(s - D_H)
+            if live(s - D_C):
+                copy_out(s - D_C)
+            if live(s - D_Q):
+                quantise(s - D_Q)
+                mx(s - D_Q)
+            if live(s - D_T):
+                transposes(s - D_T)
+            if live(s) and not on_g(s):
                 mul_w(s)
-                sumsq(s)
+            if live(s - D_S):
+                sumsq(s - D_S)
             if live(e) and e % GA == GA - 1:
                 chain_v(e // GA)
-            if live(s - D_Q):
-                threshold(s - D_Q)
             if live(s - D_N):
                 normalise(s - D_N)
+            for h in range(nh):
+                bg = s + G_AHEAD - h
+                if live(bg) and on_g(bg):
+                    mul_w_g(bg, h)

@@ -158,7 +158,10 @@ def tile_simmetricblock_t_kernel(tc, x, w, out):
             xt = xt_tiles[b]
             grouped = grp.tile([P, nn, nt], BF16, align_bytes=64)
             gr_tiles[b] = grouped
-            nc.scalar.copy(out=grouped[:], in_=xt[:].rearrange("p t r -> p r t"))
+            if b % 2 == 1:
+                nc.vector.tensor_copy(out=grouped[:], in_=xt[:].rearrange("p t r -> p r t"))
+            else:
+                nc.scalar.copy(out=grouped[:], in_=xt[:].rearrange("p t r -> p r t"))
 
         mx_tiles = {}
 

@@ -23,16 +23,14 @@ GA = 2
 STORE_B = 2
 D_S = 1
 D_CH = 2
-D_N = 3
+D_NV = 3
+D_NS = 4
 D_T = 5
 D_C = 6
 D_Q = 7
 D_H = 8
+V_TILES = (0,)
 MANUAL = True
-G_MOD = 5
-G_RES = (1, 3)
-G_AHEAD = 3
-W_PSUM = True
 
 
 def tile_simmetricblock_t_kernel(tc, x, w, out):
@@ -43,15 +41,14 @@ def tile_simmetricblock_t_kernel(tc, x, w, out):
     with ExitStack() as ctx:
         const = ctx.enter_context(tc.tile_pool(name="const", bufs=1))
         xin = ctx.enter_context(tc.tile_pool(name="xin", bufs=nb // LOAD_B))
-        xwp = ctx.enter_context(tc.tile_pool(name="xwp", bufs=14))
+        xwp = ctx.enter_context(tc.tile_pool(name="xwp", bufs=10))
         junkp = ctx.enter_context(tc.tile_pool(name="junkp", bufs=2))
         xnp = ctx.enter_context(tc.tile_pool(name="xnp", bufs=4))
         grp = ctx.enter_context(tc.tile_pool(name="grp", bufs=3))
         mxp = ctx.enter_context(tc.tile_pool(name="mxp", bufs=3))
         qp = ctx.enter_context(tc.tile_pool(name="qp", bufs=3))
         op = ctx.enter_context(tc.tile_pool(name="op", bufs=3))
-        psw = ctx.enter_context(tc.psum_pool(name="psw", bufs=1))
-        pst = ctx.enter_context(tc.psum_pool(name="pst", bufs=3))
+        pst = ctx.enter_context(tc.psum_pool(name="pst", bufs=4))
         psa = ctx.enter_context(tc.psum_pool(name="psa", bufs=4))
         if MANUAL:
             ctx.enter_context(tc.manual_schedule())
@@ -78,14 +75,7 @@ def tile_simmetricblock_t_kernel(tc, x, w, out):
             )
             x_tiles.append(x_sb)
 
-        if W_PSUM:
-            w_use = psw.tile([P, nh, nf], BF16)
-            for h in range(nh):
-                nc.tensor.matmul(
-                    out=w_use[:, h, :], lhsT=ident[:], rhs=w_sb[:, h, :], start=True, stop=True
-                )
-        else:
-            w_use = w_sb
+        w_use = w_sb
 
         xw_tiles = {}
         xn_tiles = {}
@@ -93,23 +83,10 @@ def tile_simmetricblock_t_kernel(tc, x, w, out):
         gr_tiles = {}
         o_tiles = {}
 
-        def on_g(b):
-            return b >= G_AHEAD and b % G_MOD in G_RES
-
-        def mul_w_g(b, h):
-            x_sb = x_tiles[b // LOAD_B]
-            i = b % LOAD_B
-            if h == 0:
-                xw_new = xwp.tile([P, nh, nf], F32, name="xw")
-                xw_tiles[b] = xw_new
-            nc.gpsimd.tensor_tensor(
-                out=xw_tiles[b][:, h, :], in0=x_sb[:, i * nh + h, :], in1=w_sb[:, h, :], op=ALU.mult
-            )
-
         def mul_w(b):
             x_sb = x_tiles[b // LOAD_B]
             i = b % LOAD_B
-            xw = xwp.tile([P, nh, nf], F32, name="xw")
+            xw = xwp.tile([P, nh, nf], F32)
             xw_tiles[b] = xw
             nc.vector.tensor_tensor(
                 out=xw[:], in0=x_sb[:, i * nh : (i + 1) * nh, :], in1=w_use[:], op=ALU.mult
@@ -133,16 +110,26 @@ def tile_simmetricblock_t_kernel(tc, x, w, out):
             nc.vector.tensor_scalar_max(out=nrc[:, cols], in0=nrm[:, cols], scalar1=EPS)
             nc.vector.reciprocal(out=rinv[:, cols], in_=nrc[:, cols])
 
-        def normalise(b):
+        def normalise_v(b):
             xw = xw_tiles[b]
             xn = xnp.tile([P, nh, nf], BF16)
             xn_tiles[b] = xn
-            for h in range(nh):
+            for h in V_TILES:
                 j = b * nh + h
-                nc.gpsimd.tensor_scalar(
+                nc.vector.tensor_scalar(
                     out=xn[:, h, :], in0=xw[:, h, :], scalar1=rinv[:, j : j + 1],
-                    scalar2=0.0, op0=ALU.mult, op1=ALU.add,
+                    scalar2=None, op0=ALU.mult,
                 )
+
+        def normalise_s(b):
+            xw = xw_tiles[b]
+            xn = xn_tiles[b]
+            for h in range(nh):
+                if h not in V_TILES:
+                    j = b * nh + h
+                    nc.scalar.activation(
+                        out=xn[:, h, :], in_=xw[:, h, :], func=ACT.Copy, scale=rinv[:, j : j + 1]
+                    )
 
         def transposes(b):
             xn = xn_tiles[b]
@@ -158,10 +145,7 @@ def tile_simmetricblock_t_kernel(tc, x, w, out):
             xt = xt_tiles[b]
             grouped = grp.tile([P, nn, nt], BF16, align_bytes=64)
             gr_tiles[b] = grouped
-            if b % 2 == 1:
-                nc.vector.tensor_copy(out=grouped[:], in_=xt[:].rearrange("p t r -> p r t"))
-            else:
-                nc.scalar.copy(out=grouped[:], in_=xt[:].rearrange("p t r -> p r t"))
+            nc.scalar.copy(out=grouped[:], in_=xt[:].rearrange("p t r -> p r t"))
 
         mx_tiles = {}
 
@@ -226,20 +210,18 @@ def tile_simmetricblock_t_kernel(tc, x, w, out):
                 threshold(s - D_H)
             if live(s - D_C):
                 copy_out(s - D_C)
+            if live(s - D_NS):
+                normalise_s(s - D_NS)
             if live(s - D_Q):
                 quantise(s - D_Q)
                 mx(s - D_Q)
             if live(s - D_T):
                 transposes(s - D_T)
-            if live(s) and not on_g(s):
+            if live(s):
                 mul_w(s)
             if live(s - D_S):
                 sumsq(s - D_S)
             if live(e) and e % GA == GA - 1:
                 chain_v(e // GA)
-            if live(s - D_N):
-                normalise(s - D_N)
-            for h in range(nh):
-                bg = s + G_AHEAD - h
-                if live(bg) and on_g(bg):
-                    mul_w_g(bg, h)
+            if live(s - D_NV):
+                normalise_v(s - D_NV)

@@ -23,14 +23,14 @@ GA = 2
 STORE_B = 2
 D_S = 1
 D_CH = 2
-D_NV = 3
-D_NS = 4
+D_N = 3
 D_T = 5
 D_C = 6
 D_Q = 7
-D_H = 8
-V_TILES = (0,)
+D_M = 8
+D_H = 9
 MANUAL = True
+W_PSUM = True
 
 
 def tile_simmetricblock_t_kernel(tc, x, w, out):
@@ -48,7 +48,8 @@ def tile_simmetricblock_t_kernel(tc, x, w, out):
         mxp = ctx.enter_context(tc.tile_pool(name="mxp", bufs=3))
         qp = ctx.enter_context(tc.tile_pool(name="qp", bufs=3))
         op = ctx.enter_context(tc.tile_pool(name="op", bufs=3))
-        pst = ctx.enter_context(tc.psum_pool(name="pst", bufs=4))
+        psw = ctx.enter_context(tc.psum_pool(name="psw", bufs=1))
+        pst = ctx.enter_context(tc.psum_pool(name="pst", bufs=3))
         psa = ctx.enter_context(tc.psum_pool(name="psa", bufs=4))
         if MANUAL:
             ctx.enter_context(tc.manual_schedule())
@@ -75,7 +76,14 @@ def tile_simmetricblock_t_kernel(tc, x, w, out):
             )
             x_tiles.append(x_sb)
 
-        w_use = w_sb
+        if W_PSUM:
+            w_use = psw.tile([P, nh, nf], BF16)
+            for h in range(nh):
+                nc.tensor.matmul(
+                    out=w_use[:, h, :], lhsT=ident[:], rhs=w_sb[:, h, :], start=True, stop=True
+                )
+        else:
+            w_use = w_sb
 
         xw_tiles = {}
         xn_tiles = {}
@@ -105,31 +113,24 @@ def tile_simmetricblock_t_kernel(tc, x, w, out):
             cols = slice(g * GA * nh, (g + 1) * GA * nh)
             nc.scalar.activation(out=nrm[:, cols], in_=ss[:, cols], func=ACT.Sqrt)
 
-        def chain_v(g):
+        def chain_max(g):
             cols = slice(g * GA * nh, (g + 1) * GA * nh)
             nc.vector.tensor_scalar_max(out=nrc[:, cols], in0=nrm[:, cols], scalar1=EPS)
+
+        def chain_rec(g):
+            cols = slice(g * GA * nh, (g + 1) * GA * nh)
             nc.vector.reciprocal(out=rinv[:, cols], in_=nrc[:, cols])
 
-        def normalise_v(b):
+        def normalise(b):
             xw = xw_tiles[b]
             xn = xnp.tile([P, nh, nf], BF16)
             xn_tiles[b] = xn
-            for h in V_TILES:
-                j = b * nh + h
-                nc.vector.tensor_scalar(
-                    out=xn[:, h, :], in0=xw[:, h, :], scalar1=rinv[:, j : j + 1],
-                    scalar2=None, op0=ALU.mult,
-                )
-
-        def normalise_s(b):
-            xw = xw_tiles[b]
-            xn = xn_tiles[b]
             for h in range(nh):
-                if h not in V_TILES:
-                    j = b * nh + h
-                    nc.scalar.activation(
-                        out=xn[:, h, :], in_=xw[:, h, :], func=ACT.Copy, scale=rinv[:, j : j + 1]
-                    )
+                j = b * nh + h
+                nc.gpsimd.tensor_scalar(
+                    out=xn[:, h, :], in0=xw[:, h, :], scalar1=rinv[:, j : j + 1],
+                    scalar2=0.0, op0=ALU.mult, op1=ALU.add,
+                )
 
         def transposes(b):
             xn = xn_tiles[b]
@@ -176,12 +177,19 @@ def tile_simmetricblock_t_kernel(tc, x, w, out):
                     stop=True,
                 )
 
-        def threshold(b):
+        q_tiles = {}
+
+        def mask(b):
             accf = acc_tiles[b][:].rearrange("p m j -> p (m j)")
             q = qp.tile([P, nh * nn], F32)
+            q_tiles[b] = q
             nc.vector.tensor_scalar(
                 out=q[:], in0=accf, scalar1=EMP, scalar2=ZERO / EMP, op0=ALU.is_gt, op1=ALU.max
             )
+
+        def apply(b):
+            accf = acc_tiles[b][:].rearrange("p m j -> p (m j)")
+            q = q_tiles[b]
             s = b // STORE_B
             i = b % STORE_B
             if i == 0:
@@ -202,26 +210,31 @@ def tile_simmetricblock_t_kernel(tc, x, w, out):
         def live(b):
             return 0 <= b < nb
 
+        def group_end(e):
+            return live(e) and e % GA == GA - 1
+
         for s in range(nb + D_H + 1):
-            e = s - D_CH
-            if live(e) and e % GA == GA - 1:
-                chain_s(e // GA)
-            if live(s - D_H):
-                threshold(s - D_H)
-            if live(s - D_C):
-                copy_out(s - D_C)
-            if live(s - D_NS):
-                normalise_s(s - D_NS)
-            if live(s - D_Q):
-                quantise(s - D_Q)
-                mx(s - D_Q)
+            if live(s - D_M):
+                mx(s - D_M)
             if live(s - D_T):
                 transposes(s - D_T)
+            if live(s - D_H):
+                mask(s - D_H)
             if live(s):
                 mul_w(s)
+            if group_end(s - D_CH):
+                chain_max((s - D_CH) // GA)
+            if live(s - D_H):
+                apply(s - D_H)
+            if group_end(s - D_CH):
+                chain_rec((s - D_CH) // GA)
+            if live(s - D_Q):
+                quantise(s - D_Q)
             if live(s - D_S):
                 sumsq(s - D_S)
-            if live(e) and e % GA == GA - 1:
-                chain_v(e // GA)
-            if live(s - D_NV):
-                normalise_v(s - D_NV)
+            if live(s - D_C):
+                copy_out(s - D_C)
+            if group_end(s - D_S):
+                chain_s((s - D_S) // GA)
+            if live(s - D_N):
+                normalise(s - D_N)

@@ -38,6 +38,7 @@ def tile_simmetricblock_t_kernel(tc, x, w, out):
     nb, nn, nf = x.shape
     nh = nn // P
     nt = nf // P
+    nu = nt // 2
     with ExitStack() as ctx:
         const = ctx.enter_context(tc.tile_pool(name="const", bufs=1))
         xin = ctx.enter_context(tc.tile_pool(name="xin", bufs=nb // LOAD_B))
@@ -60,6 +61,8 @@ def tile_simmetricblock_t_kernel(tc, x, w, out):
         nc.scalar.activation(out=warm[:], in_=one[:], func=ACT.Sqrt)
         ident = const.tile([P, P], BF16)
         make_identity(nc, ident[:])
+        ident_w = const.tile([P, P], F32)
+        make_identity(nc, ident_w[:])
         w_sb = const.tile([P, nh, nf], BF16)
         nc.sync.dma_start(out=w_sb[:], in_=w.rearrange("o (h p) k -> p (o h) k", p=P))
         ss = const.tile([P, nb * nh], F32)
@@ -134,19 +137,20 @@ def tile_simmetricblock_t_kernel(tc, x, w, out):
 
         def transposes(b):
             xn = xn_tiles[b]
-            xt = pst.tile([P, nt, nn], BF16)
+            words = xn[:].bitcast(F32)
+            xt = pst.tile([P, nu, nn], F32)
             xt_tiles[b] = xt
             for h in range(nh):
-                for t in range(nt):
+                for u in range(nu):
                     nc.tensor.transpose(
-                        xt[:, t, h * P : (h + 1) * P], xn[:, h, t * P : (t + 1) * P], ident[:]
+                        xt[:, u, h * P : (h + 1) * P], words[:, h, u * P : (u + 1) * P], ident_w[:]
                     )
 
         def copy_out(b):
             xt = xt_tiles[b]
             grouped = grp.tile([P, nn, nt], BF16, align_bytes=64)
             gr_tiles[b] = grouped
-            nc.scalar.copy(out=grouped[:], in_=xt[:].rearrange("p t r -> p r t"))
+            nc.scalar.copy(out=grouped[:].bitcast(F32), in_=xt[:].rearrange("p u r -> p r u"))
 
         mx_tiles = {}
 

@@ -29,6 +29,8 @@ D_C = 6
 D_Q = 7
 D_M = 8
 D_H = 9
+D_R = 10
+D_L = 11
 MANUAL = True
 W_PSUM = True
 
@@ -50,7 +52,8 @@ def tile_simmetricblock_t_kernel(tc, x, w, out):
         qp = ctx.enter_context(tc.tile_pool(name="qp", bufs=3))
         op = ctx.enter_context(tc.tile_pool(name="op", bufs=3))
         psw = ctx.enter_context(tc.psum_pool(name="psw", bufs=1))
-        pst = ctx.enter_context(tc.psum_pool(name="pst", bufs=3))
+        pst = ctx.enter_context(tc.psum_pool(name="pst", bufs=2))
+        psb = ctx.enter_context(tc.psum_pool(name="psb", bufs=1))
         psa = ctx.enter_context(tc.psum_pool(name="psa", bufs=4))
         if MANUAL:
             ctx.enter_context(tc.manual_schedule())
@@ -168,48 +171,70 @@ def tile_simmetricblock_t_kernel(tc, x, w, out):
 
         def mx(b):
             codes, scl = mx_tiles[b]
-            acc = psa.tile([P, nh, nn], F32)
+            acc = psa.tile([P, 3 * P], F32)
             acc_tiles[b] = acc
-            for m in range(nh):
-                nc.tensor.matmul_mx(
-                    out=acc[:, m, :],
-                    lhsT=codes[:, m * P : (m + 1) * P].bitcast(FP8X4),
-                    lhsT_scale=scl[:, m * P : (m + 1) * P],
-                    rhs=codes[:].bitcast(FP8X4),
-                    rhs_scale=scl[:],
-                    start=True,
-                    stop=True,
-                )
+            nc.tensor.matmul_mx(
+                out=acc[:, 0:P],
+                lhsT=codes[:, P:nn].bitcast(FP8X4),
+                lhsT_scale=scl[:, P:nn],
+                rhs=codes[:, P:nn].bitcast(FP8X4),
+                rhs_scale=scl[:, P:nn],
+                start=True,
+                stop=True,
+            )
+            nc.tensor.matmul_mx(
+                out=acc[:, P : 3 * P],
+                lhsT=codes[:, 0:P].bitcast(FP8X4),
+                lhsT_scale=scl[:, 0:P],
+                rhs=codes[:].bitcast(FP8X4),
+                rhs_scale=scl[:],
+                start=True,
+                stop=True,
+            )
 
         q_tiles = {}
 
         def mask(b):
-            accf = acc_tiles[b][:].rearrange("p m j -> p (m j)")
-            q = qp.tile([P, nh * nn], F32)
+            q = qp.tile([P, 3 * P], F32)
             q_tiles[b] = q
             nc.vector.tensor_scalar(
-                out=q[:], in0=accf, scalar1=EMP, scalar2=ZERO / EMP, op0=ALU.is_gt, op1=ALU.max
+                out=q[:], in0=acc_tiles[b][:], scalar1=EMP, scalar2=ZERO / EMP,
+                op0=ALU.is_gt, op1=ALU.max,
             )
 
         def apply(b):
-            accf = acc_tiles[b][:].rearrange("p m j -> p (m j)")
-            q = q_tiles[b]
             s = b // STORE_B
             i = b % STORE_B
             if i == 0:
-                o_new = op.tile([P, STORE_B, nh * nn], F32)
+                o_new = op.tile([P, STORE_B, 4 * P], F32)
                 o_tiles[s] = o_new
-            o_sb = o_tiles[s]
             nc.vector.scalar_tensor_tensor(
-                out=o_sb[:, i, :], in0=accf, scalar=EMP, in1=q[:], op0=ALU.max, op1=ALU.mult
+                out=o_tiles[s][:, i, P : 4 * P], in0=acc_tiles[b][:], scalar=EMP,
+                in1=q_tiles[b][:], op0=ALU.max, op1=ALU.mult,
             )
             if i == STORE_B - 1:
-                nc.sync.dma_start(
-                    out=out[s * STORE_B : (s + 1) * STORE_B].rearrange(
-                        "b (m p) j -> p (b m) j", p=P
-                    ),
-                    in_=o_sb[:].rearrange("p b (m j) -> p (b m) j", m=nh),
-                )
+                store(s, 0)
+
+        r_tiles = {}
+
+        def mirror(s):
+            r = psb.tile([P, STORE_B, P], F32)
+            r_tiles[s] = r
+            for i in range(STORE_B):
+                nc.tensor.transpose(r[:, i, :], o_tiles[s][:, i, 3 * P : 4 * P], ident_w[:])
+
+        def mirror_out(s):
+            nc.scalar.copy(out=o_tiles[s][:, :, 0:P], in_=r_tiles[s][:])
+            store(s, 1)
+
+        def store(s, m):
+            c0 = (1 - m) * nn
+            nc.sync.dma_start(
+                out=out[s * STORE_B : (s + 1) * STORE_B, m * P : (m + 1) * P, :].rearrange(
+                    "b p j -> p b j"
+                ),
+                in_=o_tiles[s][:, :, c0 : c0 + nn],
+            )
 
         def live(b):
             return 0 <= b < nb
@@ -217,11 +242,16 @@ def tile_simmetricblock_t_kernel(tc, x, w, out):
         def group_end(e):
             return live(e) and e % GA == GA - 1
 
-        for s in range(nb + D_H + 1):
+        def store_end(e):
+            return live(e) and e % STORE_B == STORE_B - 1
+
+        for s in range(nb + D_L + 1):
             if live(s - D_M):
                 mx(s - D_M)
             if live(s - D_T):
                 transposes(s - D_T)
+            if store_end(s - D_R):
+                mirror((s - D_R) // STORE_B)
             if live(s - D_H):
                 mask(s - D_H)
             if live(s):
@@ -238,6 +268,8 @@ def tile_simmetricblock_t_kernel(tc, x, w, out):
                 sumsq(s - D_S)
             if live(s - D_C):
                 copy_out(s - D_C)
+            if store_end(s - D_L):
+                mirror_out((s - D_L) // STORE_B)
             if group_end(s - D_S):
                 chain_s((s - D_S) // GA)
             if live(s - D_N):

@@ -17,10 +17,18 @@ P = 128
 EMP = 0.1
 EPS = 1e-8
 ZERO = 9e-15
+STEEP = 2.0 ** 100
+MODG = lambda b: False
+MODS = lambda b: False
+SINGLE = 30
+TV = False
+DV = lambda b: False
+CS = lambda b, h: False
+CVV = lambda b, h: False
 
 LOAD_B = 2
 GA = 2
-STORE_B = 2
+STORE_B = 4
 D_S = 1
 D_CH = 2
 D_N = 3
@@ -28,6 +36,8 @@ D_T = 5
 D_C = 6
 D_Q = 7
 D_M = 8
+D_F = 9
+D_G = 10
 D_H = 9
 D_R = 10
 D_L = 11
@@ -43,14 +53,15 @@ def tile_simmetricblock_t_kernel(tc, x, w, out):
     nu = nt // 2
     with ExitStack() as ctx:
         const = ctx.enter_context(tc.tile_pool(name="const", bufs=1))
-        xin = ctx.enter_context(tc.tile_pool(name="xin", bufs=nb // LOAD_B))
+        xin = ctx.enter_context(tc.tile_pool(name="xin", bufs=nb // LOAD_B + 1))
         xwp = ctx.enter_context(tc.tile_pool(name="xwp", bufs=10))
         junkp = ctx.enter_context(tc.tile_pool(name="junkp", bufs=2))
         xnp = ctx.enter_context(tc.tile_pool(name="xnp", bufs=4))
         grp = ctx.enter_context(tc.tile_pool(name="grp", bufs=3))
         mxp = ctx.enter_context(tc.tile_pool(name="mxp", bufs=3))
         qp = ctx.enter_context(tc.tile_pool(name="qp", bufs=3))
-        op = ctx.enter_context(tc.tile_pool(name="op", bufs=3))
+        cp = ctx.enter_context(tc.tile_pool(name="cp", bufs=3))
+        op = ctx.enter_context(tc.tile_pool(name="op", bufs=4))
         psw = ctx.enter_context(tc.psum_pool(name="psw", bufs=1))
         pst = ctx.enter_context(tc.psum_pool(name="pst", bufs=2))
         psb = ctx.enter_context(tc.psum_pool(name="psb", bufs=1))
@@ -66,6 +77,12 @@ def tile_simmetricblock_t_kernel(tc, x, w, out):
         make_identity(nc, ident[:])
         ident_w = const.tile([P, P], F32)
         make_identity(nc, ident_w[:])
+        thr = const.tile([P, 1], F32)
+        nc.vector.tensor_scalar(
+            out=thr[:], in0=one[:], scalar1=-EMP * STEEP, scalar2=None, op0=ALU.mult
+        )
+        flo = const.tile([P, 1], F32)
+        nc.vector.tensor_scalar(out=flo[:], in0=one[:], scalar1=ZERO, scalar2=None, op0=ALU.mult)
         w_sb = const.tile([P, nh, nf], BF16)
         nc.sync.dma_start(out=w_sb[:], in_=w.rearrange("o (h p) k -> p (o h) k", p=P))
         ss = const.tile([P, nb * nh], F32)
@@ -73,14 +90,18 @@ def tile_simmetricblock_t_kernel(tc, x, w, out):
         nrc = const.tile([P, nb * nh], F32)
         rinv = const.tile([P, nb * nh], F32)
 
-        x_tiles = []
-        for l in range(nb // LOAD_B):
+        x_tiles = {}
+        b = 0
+        while b < nb:
+            n = 1 if b < LOAD_B else LOAD_B
             x_sb = xin.tile([P, LOAD_B * nh, nf], BF16)
             nc.sync.dma_start(
-                out=x_sb[:],
-                in_=x[l * LOAD_B : (l + 1) * LOAD_B].rearrange("b (h p) k -> p (b h) k", p=P),
+                out=x_sb[:, 0 : n * nh, :],
+                in_=x[b : b + n].rearrange("b (h p) k -> p (b h) k", p=P),
             )
-            x_tiles.append(x_sb)
+            for i in range(n):
+                x_tiles[b + i] = x_sb[:, i * nh : (i + 1) * nh, :]
+            b += n
 
         if W_PSUM:
             w_use = psw.tile([P, nh, nf], BF16)
@@ -98,12 +119,10 @@ def tile_simmetricblock_t_kernel(tc, x, w, out):
         o_tiles = {}
 
         def mul_w(b):
-            x_sb = x_tiles[b // LOAD_B]
-            i = b % LOAD_B
             xw = xwp.tile([P, nh, nf], F32)
             xw_tiles[b] = xw
             nc.vector.tensor_tensor(
-                out=xw[:], in0=x_sb[:, i * nh : (i + 1) * nh, :], in1=w_use[:], op=ALU.mult
+                out=xw[:], in0=x_tiles[b], in1=w_use[:], op=ALU.mult
             )
 
         def sumsq(b):
@@ -127,16 +146,28 @@ def tile_simmetricblock_t_kernel(tc, x, w, out):
             cols = slice(g * GA * nh, (g + 1) * GA * nh)
             nc.vector.reciprocal(out=rinv[:, cols], in_=nrc[:, cols])
 
-        def normalise(b):
+        def normalise(b, who):
             xw = xw_tiles[b]
-            xn = xnp.tile([P, nh, nf], BF16)
-            xn_tiles[b] = xn
+            if b not in xn_tiles:
+                xn = xnp.tile([P, nh, nf], BF16)
+                xn_tiles[b] = xn
+            xn = xn_tiles[b]
             for h in range(nh):
                 j = b * nh + h
-                nc.gpsimd.tensor_scalar(
-                    out=xn[:, h, :], in0=xw[:, h, :], scalar1=rinv[:, j : j + 1],
-                    scalar2=0.0, op0=ALU.mult, op1=ALU.add,
-                )
+                if who == "S" and CS(b, h):
+                    nc.scalar.activation(
+                        out=xn[:, h, :], in_=xw[:, h, :], func=ACT.Copy, scale=rinv[:, j : j + 1]
+                    )
+                if who == "V" and CVV(b, h):
+                    nc.vector.tensor_scalar(
+                        out=xn[:, h, :], in0=xw[:, h, :], scalar1=rinv[:, j : j + 1],
+                        scalar2=None, op0=ALU.mult,
+                    )
+                if who == "G" and not CS(b, h) and not CVV(b, h):
+                    nc.gpsimd.tensor_scalar(
+                        out=xn[:, h, :], in0=xw[:, h, :], scalar1=rinv[:, j : j + 1],
+                        scalar2=0.0, op0=ALU.mult, op1=ALU.add,
+                    )
 
         def transposes(b):
             xn = xn_tiles[b]
@@ -153,7 +184,8 @@ def tile_simmetricblock_t_kernel(tc, x, w, out):
             xt = xt_tiles[b]
             grouped = grp.tile([P, nn, nt], BF16, align_bytes=64)
             gr_tiles[b] = grouped
-            nc.scalar.copy(out=grouped[:].bitcast(F32), in_=xt[:].rearrange("p u r -> p r u"))
+            eng = nc.vector.tensor_copy if DV(b) else nc.scalar.copy
+            eng(out=grouped[:].bitcast(F32), in_=xt[:].rearrange("p u r -> p r u"))
 
         mx_tiles = {}
 
@@ -202,39 +234,97 @@ def tile_simmetricblock_t_kernel(tc, x, w, out):
                 op0=ALU.is_gt, op1=ALU.max,
             )
 
+        firsts = {}
+        sizes = {}
+        f = 0
+        while f < nb:
+            n = min(STORE_B, max(1, (nb - f) // 2))
+            for i in range(n):
+                firsts[f + i] = f
+                sizes[f + i] = n
+            f += n
+
+        def first(b):
+            return firsts[b]
+
+        def size(b):
+            return sizes[b]
+
+        def last(b):
+            return b == first(b) + size(b) - 1
+
         def apply(b):
-            s = b // STORE_B
-            i = b % STORE_B
-            if i == 0:
+            if b == first(b):
                 o_new = op.tile([P, STORE_B, 4 * P], F32)
-                o_tiles[s] = o_new
+                o_tiles[b] = o_new
+            o_sb = o_tiles[first(b)]
+            i = b - first(b)
+            if shared(b):
+                scalar, op0, op1 = ZERO, ALU.max, ALU.min
+            else:
+                scalar, op0, op1 = EMP, ALU.max, ALU.mult
             nc.vector.scalar_tensor_tensor(
-                out=o_tiles[s][:, i, P : 4 * P], in0=acc_tiles[b][:], scalar=EMP,
-                in1=q_tiles[b][:], op0=ALU.max, op1=ALU.mult,
+                out=o_sb[:, i, P : 4 * P], in0=acc_tiles[b][:], scalar=scalar,
+                in1=q_tiles[b][:], op0=op0, op1=op1,
             )
-            if i == STORE_B - 1:
-                store(s, 0)
+            if last(b):
+                store(b, 0)
 
         r_tiles = {}
 
-        def mirror(s):
+        def mirror(b):
             r = psb.tile([P, STORE_B, P], F32)
-            r_tiles[s] = r
-            for i in range(STORE_B):
-                nc.tensor.transpose(r[:, i, :], o_tiles[s][:, i, 3 * P : 4 * P], ident_w[:])
+            r_tiles[b] = r
+            for i in range(size(b)):
+                nc.tensor.transpose(r[:, i, :], o_tiles[first(b)][:, i, 3 * P : 4 * P], ident_w[:])
 
-        def mirror_out(s):
-            nc.scalar.copy(out=o_tiles[s][:, :, 0:P], in_=r_tiles[s][:])
-            store(s, 1)
+        def mirror_out(b):
+            n = size(b)
+            if TV:
+                nc.vector.tensor_copy(out=o_tiles[first(b)][:, 0:n, 0:P], in_=r_tiles[b][:, 0:n, :])
+            else:
+                nc.scalar.copy(out=o_tiles[first(b)][:, 0:n, 0:P], in_=r_tiles[b][:, 0:n, :])
+            store(b, 1)
 
-        def store(s, m):
+        def store(b, m):
             c0 = (1 - m) * nn
+            f = first(b)
             nc.sync.dma_start(
-                out=out[s * STORE_B : (s + 1) * STORE_B, m * P : (m + 1) * P, :].rearrange(
-                    "b p j -> p b j"
-                ),
-                in_=o_tiles[s][:, :, c0 : c0 + nn],
+                out=out[f : b + 1, m * P : (m + 1) * P, :].rearrange("b p j -> p b j"),
+                in_=o_tiles[f][:, 0 : size(b), c0 : c0 + nn],
             )
+
+        c_tiles = {}
+
+        def rise(b):
+            c = cp.tile([P, 3 * P], F32)
+            c_tiles[b] = c
+            nc.scalar.activation(
+                out=c[:], in_=acc_tiles[b][:], func=ACT.Relu, scale=STEEP, bias=thr[:]
+            )
+
+        def floor_g(b):
+            qg = cp.tile([P, 3 * P], F32)
+            q_tiles[b] = qg
+            nc.gpsimd.tensor_scalar(
+                out=qg[:], in0=c_tiles[b][:], scalar1=1.0, scalar2=ZERO, op0=ALU.mult, op1=ALU.add
+            )
+
+        def floor_s(b):
+            qs = cp.tile([P, 3 * P], F32)
+            q_tiles[b] = qs
+            nc.scalar.activation(
+                out=qs[:], in_=c_tiles[b][:], func=ACT.Identity, bias=flo[:]
+            )
+
+        def on_g(b):
+            return live(b) and MODG(b)
+
+        def on_s(b):
+            return live(b) and MODS(b)
+
+        def shared(b):
+            return on_g(b) or on_s(b)
 
         def live(b):
             return 0 <= b < nb
@@ -243,7 +333,7 @@ def tile_simmetricblock_t_kernel(tc, x, w, out):
             return live(e) and e % GA == GA - 1
 
         def store_end(e):
-            return live(e) and e % STORE_B == STORE_B - 1
+            return live(e) and last(e)
 
         for s in range(nb + D_L + 1):
             if live(s - D_M):
@@ -251,8 +341,8 @@ def tile_simmetricblock_t_kernel(tc, x, w, out):
             if live(s - D_T):
                 transposes(s - D_T)
             if store_end(s - D_R):
-                mirror((s - D_R) // STORE_B)
-            if live(s - D_H):
+                mirror(s - D_R)
+            if live(s - D_H) and not shared(s - D_H):
                 mask(s - D_H)
             if live(s):
                 mul_w(s)
@@ -262,15 +352,27 @@ def tile_simmetricblock_t_kernel(tc, x, w, out):
                 apply(s - D_H)
             if group_end(s - D_CH):
                 chain_rec((s - D_CH) // GA)
+            if live(s - D_N):
+                normalise(s - D_N, "V")
             if live(s - D_Q):
                 quantise(s - D_Q)
+            if live(s - D_C) and DV(s - D_C):
+                copy_out(s - D_C)
             if live(s - D_S):
                 sumsq(s - D_S)
-            if live(s - D_C):
+            if live(s - D_N):
+                normalise(s - D_N, "S")
+            if live(s - D_C) and not DV(s - D_C):
                 copy_out(s - D_C)
+            if shared(s - D_F):
+                rise(s - D_F)
+            if on_s(s - D_G):
+                floor_s(s - D_G)
             if store_end(s - D_L):
-                mirror_out((s - D_L) // STORE_B)
+                mirror_out(s - D_L)
             if group_end(s - D_S):
                 chain_s((s - D_S) // GA)
             if live(s - D_N):
-                normalise(s - D_N)
+                normalise(s - D_N, "G")
+            if on_g(s - D_G):
+                floor_g(s - D_G)

@@ -27,20 +27,20 @@ CS = lambda b, h: False
 CVV = lambda b, h: False
 
 LOAD_B = 2
-GA = 2
+GA = 1
 STORE_B = 4
 D_S = 1
 D_CH = 2
-D_N = 3
-D_T = 5
-D_C = 6
-D_Q = 7
-D_M = 8
-D_F = 9
-D_G = 10
-D_H = 9
-D_R = 10
-D_L = 11
+D_N = 2
+D_T = 4
+D_C = 5
+D_Q = 6
+D_M = 7
+D_F = 8
+D_G = 9
+D_H = 8
+D_R = 9
+D_L = 10
 MANUAL = True
 W_PSUM = True
 
@@ -88,6 +88,14 @@ def tile_simmetricblock_t_kernel(tc, x, w, out):
         ss = const.tile([P, nb * nh], F32)
         nrm = const.tile([P, nb * nh], F32)
         nrc = const.tile([P, nb * nh], F32)
+        eps2 = const.tile([P, 1], F32)
+        nc.vector.tensor_scalar(
+            out=eps2[:], in0=one[:], scalar1=EPS * EPS, scalar2=None, op0=ALU.mult
+        )
+        minus_eps2 = const.tile([P, 1], F32)
+        nc.vector.tensor_scalar(
+            out=minus_eps2[:], in0=one[:], scalar1=-EPS * EPS, scalar2=None, op0=ALU.mult
+        )
         rinv = const.tile([P, nb * nh], F32)
 
         x_tiles = {}
@@ -134,17 +142,19 @@ def tile_simmetricblock_t_kernel(tc, x, w, out):
                     out=junk[:], in_=xw[:, h, :], func=ACT.Square, accum_out=ss[:, j : j + 1]
                 )
 
-        def chain_s(g):
+        def chain_relu(g):
             cols = slice(g * GA * nh, (g + 1) * GA * nh)
-            nc.scalar.activation(out=nrm[:, cols], in_=ss[:, cols], func=ACT.Sqrt)
+            nc.scalar.activation(
+                out=nrc[:, cols], in_=ss[:, cols], func=ACT.Relu, bias=minus_eps2[:]
+            )
 
-        def chain_max(g):
+        def chain_sqrt(g):
             cols = slice(g * GA * nh, (g + 1) * GA * nh)
-            nc.vector.tensor_scalar_max(out=nrc[:, cols], in0=nrm[:, cols], scalar1=EPS)
+            nc.scalar.activation(out=nrm[:, cols], in_=nrc[:, cols], func=ACT.Sqrt, bias=eps2[:])
 
         def chain_rec(g):
             cols = slice(g * GA * nh, (g + 1) * GA * nh)
-            nc.vector.reciprocal(out=rinv[:, cols], in_=nrc[:, cols])
+            nc.vector.reciprocal(out=rinv[:, cols], in_=nrm[:, cols])
 
         def normalise(b, who):
             xw = xw_tiles[b]
@@ -346,20 +356,20 @@ def tile_simmetricblock_t_kernel(tc, x, w, out):
                 mask(s - D_H)
             if live(s):
                 mul_w(s)
-            if group_end(s - D_CH):
-                chain_max((s - D_CH) // GA)
             if live(s - D_H):
                 apply(s - D_H)
-            if group_end(s - D_CH):
-                chain_rec((s - D_CH) // GA)
             if live(s - D_N):
                 normalise(s - D_N, "V")
             if live(s - D_Q):
                 quantise(s - D_Q)
+            if group_end(s - D_CH):
+                chain_rec((s - D_CH) // GA)
             if live(s - D_C) and DV(s - D_C):
                 copy_out(s - D_C)
             if live(s - D_S):
                 sumsq(s - D_S)
+            if group_end(s - D_S):
+                chain_relu((s - D_S) // GA)
             if live(s - D_N):
                 normalise(s - D_N, "S")
             if live(s - D_C) and not DV(s - D_C):
@@ -371,7 +381,7 @@ def tile_simmetricblock_t_kernel(tc, x, w, out):
             if store_end(s - D_L):
                 mirror_out(s - D_L)
             if group_end(s - D_S):
-                chain_s((s - D_S) // GA)
+                chain_sqrt((s - D_S) // GA)
             if live(s - D_N):
                 normalise(s - D_N, "G")
             if on_g(s - D_G):

@@ -21,24 +21,31 @@ STEEP = 2.0 ** 100
 MODG = lambda b: False
 MODS = lambda b: False
 SINGLE = 30
+ORDER_S = "BlNDrfmq"
+SPLIT0 = True
+TAIL = True
+REC_FIRST = False
+AG = ()
+BV = lambda b, h: False
 TV = False
 DV = lambda b: False
-CS = lambda b, h: False
-CVV = lambda b, h: False
+CS = lambda b, h: b >= 30 and h == 1
+CVV = lambda b, h: b < 4 and h == 1
 
 LOAD_B = 2
 GA = 1
 STORE_B = 4
 D_S = 1
 D_CH = 2
-D_N = 2
+D_N = 3
 D_T = 4
 D_C = 5
 D_Q = 6
 D_M = 7
 D_F = 8
-D_G = 9
+D_G = 8
 D_H = 8
+D_A = 8
 D_R = 9
 D_L = 10
 MANUAL = True
@@ -84,7 +91,8 @@ def tile_simmetricblock_t_kernel(tc, x, w, out):
         flo = const.tile([P, 1], F32)
         nc.vector.tensor_scalar(out=flo[:], in0=one[:], scalar1=ZERO, scalar2=None, op0=ALU.mult)
         w_sb = const.tile([P, nh, nf], BF16)
-        nc.sync.dma_start(out=w_sb[:], in_=w.rearrange("o (h p) k -> p (o h) k", p=P))
+        if not SPLIT0:
+            nc.sync.dma_start(out=w_sb[:], in_=w.rearrange("o (h p) k -> p (o h) k", p=P))
         ss = const.tile([P, nb * nh], F32)
         nrm = const.tile([P, nb * nh], F32)
         nrc = const.tile([P, nb * nh], F32)
@@ -103,10 +111,15 @@ def tile_simmetricblock_t_kernel(tc, x, w, out):
         while b < nb:
             n = 1 if b < LOAD_B else LOAD_B
             x_sb = xin.tile([P, LOAD_B * nh, nf], BF16)
-            nc.sync.dma_start(
-                out=x_sb[:, 0 : n * nh, :],
-                in_=x[b : b + n].rearrange("b (h p) k -> p (b h) k", p=P),
-            )
+            if b == 0 and SPLIT0:
+                for h in range(nh):
+                    nc.sync.dma_start(out=w_sb[:, h, :], in_=w[0, h * P : (h + 1) * P, :])
+                    nc.sync.dma_start(out=x_sb[:, h, :], in_=x[0, h * P : (h + 1) * P, :])
+            else:
+                nc.sync.dma_start(
+                    out=x_sb[:, 0 : n * nh, :],
+                    in_=x[b : b + n].rearrange("b (h p) k -> p (b h) k", p=P),
+                )
             for i in range(n):
                 x_tiles[b + i] = x_sb[:, i * nh : (i + 1) * nh, :]
             b += n
@@ -129,15 +142,35 @@ def tile_simmetricblock_t_kernel(tc, x, w, out):
         def mul_w(b):
             xw = xwp.tile([P, nh, nf], F32)
             xw_tiles[b] = xw
-            nc.vector.tensor_tensor(
-                out=xw[:], in0=x_tiles[b], in1=w_use[:], op=ALU.mult
+            if b == 0 and SPLIT0:
+                for h in range(nh):
+                    nc.vector.tensor_tensor(
+                        out=xw[:, h, :], in0=x_tiles[b][:, h, :], in1=w_sb[:, h, :], op=ALU.mult
+                    )
+                return
+            eng = nc.gpsimd if b in AG else nc.vector
+            eng.tensor_tensor(
+                out=xw[:], in0=x_tiles[b], in1=w_sb[:] if b in AG else w_use[:], op=ALU.mult
             )
+
+        def sumsq_v(b):
+            for h in range(nh):
+                if BV(b, h):
+                    junk_v = junkp.tile([P, nf], BF16)
+                    j = b * nh + h
+                    nc.vector.scalar_tensor_tensor(
+                        out=junk_v[:], in0=xw_tiles[b][:, h, :], scalar=1.0,
+                        in1=xw_tiles[b][:, h, :], op0=ALU.mult, op1=ALU.mult,
+                        accum_out=ss[:, j : j + 1],
+                    )
 
         def sumsq(b):
             xw = xw_tiles[b]
             for h in range(nh):
                 junk = junkp.tile([P, nf], BF16)
                 j = b * nh + h
+                if BV(b, h):
+                    continue
                 nc.scalar.activation(
                     out=junk[:], in_=xw[:, h, :], func=ACT.Square, accum_out=ss[:, j : j + 1]
                 )
@@ -236,13 +269,19 @@ def tile_simmetricblock_t_kernel(tc, x, w, out):
 
         q_tiles = {}
 
+        def parts(b):
+            if TAIL and b == nb - 1:
+                return [slice(2 * P, 3 * P), slice(0, 2 * P)]
+            return [slice(0, 3 * P)]
+
         def mask(b):
             q = qp.tile([P, 3 * P], F32)
             q_tiles[b] = q
-            nc.vector.tensor_scalar(
-                out=q[:], in0=acc_tiles[b][:], scalar1=EMP, scalar2=ZERO / EMP,
-                op0=ALU.is_gt, op1=ALU.max,
-            )
+            for c in parts(b):
+                nc.vector.tensor_scalar(
+                    out=q[:, c], in0=acc_tiles[b][:, c], scalar1=EMP, scalar2=ZERO / EMP,
+                    op0=ALU.is_gt, op1=ALU.max,
+                )
 
         firsts = {}
         sizes = {}
@@ -273,10 +312,11 @@ def tile_simmetricblock_t_kernel(tc, x, w, out):
                 scalar, op0, op1 = ZERO, ALU.max, ALU.min
             else:
                 scalar, op0, op1 = EMP, ALU.max, ALU.mult
-            nc.vector.scalar_tensor_tensor(
-                out=o_sb[:, i, P : 4 * P], in0=acc_tiles[b][:], scalar=scalar,
-                in1=q_tiles[b][:], op0=op0, op1=op1,
-            )
+            for c in parts(b):
+                nc.vector.scalar_tensor_tensor(
+                    out=o_sb[:, i, P + c.start : P + c.stop], in0=acc_tiles[b][:, c], scalar=scalar,
+                    in1=q_tiles[b][:, c], op0=op0, op1=op1,
+                )
             if last(b):
                 store(b, 0)
 
@@ -345,6 +385,8 @@ def tile_simmetricblock_t_kernel(tc, x, w, out):
         def store_end(e):
             return live(e) and last(e)
 
+        for b in AG:
+            mul_w(b)
         for s in range(nb + D_L + 1):
             if live(s - D_M):
                 mx(s - D_M)
@@ -354,34 +396,41 @@ def tile_simmetricblock_t_kernel(tc, x, w, out):
                 mirror(s - D_R)
             if live(s - D_H) and not shared(s - D_H):
                 mask(s - D_H)
-            if live(s):
+            if live(s) and s not in AG:
                 mul_w(s)
-            if live(s - D_H):
-                apply(s - D_H)
+            if live(s - D_S):
+                sumsq_v(s - D_S)
+            if not live(s) and live(s - D_Q):
+                quantise(s - D_Q)
+            if live(s - D_A):
+                apply(s - D_A)
             if live(s - D_N):
                 normalise(s - D_N, "V")
-            if live(s - D_Q):
+            if group_end(s - D_CH) and REC_FIRST:
+                chain_rec((s - D_CH) // GA)
+            if live(s) and live(s - D_Q):
                 quantise(s - D_Q)
-            if group_end(s - D_CH):
+            if group_end(s - D_CH) and not REC_FIRST:
                 chain_rec((s - D_CH) // GA)
             if live(s - D_C) and DV(s - D_C):
                 copy_out(s - D_C)
-            if live(s - D_S):
-                sumsq(s - D_S)
-            if group_end(s - D_S):
-                chain_relu((s - D_S) // GA)
-            if live(s - D_N):
-                normalise(s - D_N, "S")
-            if live(s - D_C) and not DV(s - D_C):
-                copy_out(s - D_C)
-            if shared(s - D_F):
-                rise(s - D_F)
-            if on_s(s - D_G):
-                floor_s(s - D_G)
-            if store_end(s - D_L):
-                mirror_out(s - D_L)
-            if group_end(s - D_S):
-                chain_sqrt((s - D_S) // GA)
+            for k in ORDER_S:
+                if k == "B" and live(s - D_S):
+                    sumsq(s - D_S)
+                if k == "l" and group_end(s - D_S):
+                    chain_relu((s - D_S) // GA)
+                if k == "q" and group_end(s - D_S):
+                    chain_sqrt((s - D_S) // GA)
+                if k == "N" and live(s - D_N):
+                    normalise(s - D_N, "S")
+                if k == "D" and live(s - D_C) and not DV(s - D_C):
+                    copy_out(s - D_C)
+                if k == "r" and shared(s - D_F):
+                    rise(s - D_F)
+                if k == "f" and on_s(s - D_G):
+                    floor_s(s - D_G)
+                if k == "m" and store_end(s - D_L):
+                    mirror_out(s - D_L)
             if live(s - D_N):
                 normalise(s - D_N, "G")
             if on_g(s - D_G):

@@ -21,7 +21,7 @@ STEEP = 2.0 ** 100
 MODG = lambda b: False
 MODS = lambda b: False
 SINGLE = 30
-ORDER_S = "BlNDrfmq"
+ORDER_S = "BDlNmq"
 SPLIT0 = True
 TAIL = True
 REC_FIRST = False
@@ -29,7 +29,7 @@ AG = ()
 BV = lambda b, h: False
 TV = False
 DV = lambda b: False
-CS = lambda b, h: b >= 30 and h == 1
+CS = lambda b, h: b >= 28 and h == 1
 CVV = lambda b, h: b < 4 and h == 1
 
 LOAD_B = 2
@@ -164,9 +164,9 @@ def tile_simmetricblock_t_kernel(tc, x, w, out):
                         accum_out=ss[:, j : j + 1],
                     )
 
-        def sumsq(b):
+        def sumsq(b, hs=(0, 1)):
             xw = xw_tiles[b]
-            for h in range(nh):
+            for h in hs:
                 junk = junkp.tile([P, nf], BF16)
                 j = b * nh + h
                 if BV(b, h):
@@ -417,10 +417,18 @@ def tile_simmetricblock_t_kernel(tc, x, w, out):
             for k in ORDER_S:
                 if k == "B" and live(s - D_S):
                     sumsq(s - D_S)
+                if k == "b" and live(s - D_S):
+                    sumsq(s - D_S, (0,))
+                if k == "c" and live(s - D_S):
+                    sumsq(s - D_S, (1,))
                 if k == "l" and group_end(s - D_S):
                     chain_relu((s - D_S) // GA)
                 if k == "q" and group_end(s - D_S):
                     chain_sqrt((s - D_S) // GA)
+                if k == "L" and group_end(s - D_S - 1):
+                    chain_relu((s - D_S - 1) // GA)
+                if k == "Q" and group_end(s - D_S - 1):
+                    chain_sqrt((s - D_S - 1) // GA)
                 if k == "N" and live(s - D_N):
                     normalise(s - D_N, "S")
                 if k == "D" and live(s - D_C) and not DV(s - D_C):

from contextlib import ExitStack

import concourse.mybir as mybir
from concourse.masks import make_identity

FLOPS = 2 * 32 * 256 * 256 * 512

F32 = mybir.dt.float32
BF16 = mybir.dt.bfloat16
U32 = mybir.dt.uint32
U8 = mybir.dt.uint8
FP8X4 = mybir.dt.float8_e4m3fn_x4
ALU = mybir.AluOpType
ACT = mybir.ActivationFunctionType

P = 128
EMP = 0.1
EPS = 1e-8
ZERO = 9e-15
STEEP = 2.0 ** 100
MODG = lambda b: False
MODS = lambda b: False
SINGLE = 30
ORDER_S = "BDlNmq"
SPLIT0 = True
TAIL = True
REC_FIRST = False
AG = ()
BV = lambda b, h: False
TV = False
DV = lambda b: False
CS = lambda b, h: b >= 28 and h == 1
CVV = lambda b, h: b < 4 and h == 1

LOAD_B = 2
GA = 1
STORE_B = 4
D_S = 1
D_CH = 2
D_N = 3
D_T = 4
D_C = 5
D_Q = 6
D_M = 7
D_F = 8
D_G = 8
D_H = 8
D_A = 8
D_R = 9
D_L = 10
MANUAL = True
W_PSUM = True


def tile_simmetricblock_t_kernel(tc, x, w, out):
    nc = tc.nc
    nb, nn, nf = x.shape
    nh = nn // P
    nt = nf // P
    nu = nt // 2
    with ExitStack() as ctx:
        const = ctx.enter_context(tc.tile_pool(name="const", bufs=1))
        xin = ctx.enter_context(tc.tile_pool(name="xin", bufs=nb // LOAD_B + 1))
        xwp = ctx.enter_context(tc.tile_pool(name="xwp", bufs=10))
        junkp = ctx.enter_context(tc.tile_pool(name="junkp", bufs=2))
        xnp = ctx.enter_context(tc.tile_pool(name="xnp", bufs=4))
        grp = ctx.enter_context(tc.tile_pool(name="grp", bufs=3))
        mxp = ctx.enter_context(tc.tile_pool(name="mxp", bufs=3))
        qp = ctx.enter_context(tc.tile_pool(name="qp", bufs=3))
        cp = ctx.enter_context(tc.tile_pool(name="cp", bufs=3))
        op = ctx.enter_context(tc.tile_pool(name="op", bufs=4))
        psw = ctx.enter_context(tc.psum_pool(name="psw", bufs=1))
        pst = ctx.enter_context(tc.psum_pool(name="pst", bufs=2))
        psb = ctx.enter_context(tc.psum_pool(name="psb", bufs=1))
        psa = ctx.enter_context(tc.psum_pool(name="psa", bufs=4))
        if MANUAL:
            ctx.enter_context(tc.manual_schedule())

        one = const.tile([P, 1], F32)
        nc.vector.memset(one[:], 1.0)
        warm = const.tile([P, 1], F32)
        nc.scalar.activation(out=warm[:], in_=one[:], func=ACT.Sqrt)
        ident = const.tile([P, P], BF16)
        make_identity(nc, ident[:])
        ident_w = const.tile([P, P], F32)
        make_identity(nc, ident_w[:])
        thr = const.tile([P, 1], F32)
        nc.vector.tensor_scalar(
            out=thr[:], in0=one[:], scalar1=-EMP * STEEP, scalar2=None, op0=ALU.mult
        )
        flo = const.tile([P, 1], F32)
        nc.vector.tensor_scalar(out=flo[:], in0=one[:], scalar1=ZERO, scalar2=None, op0=ALU.mult)
        w_sb = const.tile([P, nh, nf], BF16)
        if not SPLIT0:
            nc.sync.dma_start(out=w_sb[:], in_=w.rearrange("o (h p) k -> p (o h) k", p=P))
        ss = const.tile([P, nb * nh], F32)
        nrm = const.tile([P, nb * nh], F32)
        nrc = const.tile([P, nb * nh], F32)
        eps2 = const.tile([P, 1], F32)
        nc.vector.tensor_scalar(
            out=eps2[:], in0=one[:], scalar1=EPS * EPS, scalar2=None, op0=ALU.mult
        )
        minus_eps2 = const.tile([P, 1], F32)
        nc.vector.tensor_scalar(
            out=minus_eps2[:], in0=one[:], scalar1=-EPS * EPS, scalar2=None, op0=ALU.mult
        )
        rinv = const.tile([P, nb * nh], F32)

        x_tiles = {}
        b = 0
        while b < nb:
            n = 1 if b < LOAD_B else LOAD_B
            x_sb = xin.tile([P, LOAD_B * nh, nf], BF16)
            if b == 0 and SPLIT0:
                for h in range(nh):
                    nc.sync.dma_start(out=w_sb[:, h, :], in_=w[0, h * P : (h + 1) * P, :])
                    nc.sync.dma_start(out=x_sb[:, h, :], in_=x[0, h * P : (h + 1) * P, :])
            else:
                nc.sync.dma_start(
                    out=x_sb[:, 0 : n * nh, :],
                    in_=x[b : b + n].rearrange("b (h p) k -> p (b h) k", p=P),
                )
            for i in range(n):
                x_tiles[b + i] = x_sb[:, i * nh : (i + 1) * nh, :]
            b += n

        if W_PSUM:
            w_use = psw.tile([P, nh, nf], BF16)
            for h in range(nh):
                nc.tensor.matmul(
                    out=w_use[:, h, :], lhsT=ident[:], rhs=w_sb[:, h, :], start=True, stop=True
                )
        else:
            w_use = w_sb

        xw_tiles = {}
        xn_tiles = {}
        xt_tiles = {}
        gr_tiles = {}
        o_tiles = {}

        def mul_w(b):
            xw = xwp.tile([P, nh, nf], F32)
            xw_tiles[b] = xw
            if b == 0 and SPLIT0:
                for h in range(nh):
                    nc.vector.tensor_tensor(
                        out=xw[:, h, :], in0=x_tiles[b][:, h, :], in1=w_sb[:, h, :], op=ALU.mult
                    )
                return
            eng = nc.gpsimd if b in AG else nc.vector
            eng.tensor_tensor(
                out=xw[:], in0=x_tiles[b], in1=w_sb[:] if b in AG else w_use[:], op=ALU.mult
            )

        def sumsq_v(b):
            for h in range(nh):
                if BV(b, h):
                    junk_v = junkp.tile([P, nf], BF16)
                    j = b * nh + h
                    nc.vector.scalar_tensor_tensor(
                        out=junk_v[:], in0=xw_tiles[b][:, h, :], scalar=1.0,
                        in1=xw_tiles[b][:, h, :], op0=ALU.mult, op1=ALU.mult,
                        accum_out=ss[:, j : j + 1],
                    )

        def sumsq(b, hs=(0, 1)):
            xw = xw_tiles[b]
            for h in hs:
                junk = junkp.tile([P, nf], BF16)
                j = b * nh + h
                if BV(b, h):
                    continue
                nc.scalar.activation(
                    out=junk[:], in_=xw[:, h, :], func=ACT.Square, accum_out=ss[:, j : j + 1]
                )

        def chain_relu(g):
            cols = slice(g * GA * nh, (g + 1) * GA * nh)
            nc.scalar.activation(
                out=nrc[:, cols], in_=ss[:, cols], func=ACT.Relu, bias=minus_eps2[:]
            )

        def chain_sqrt(g):
            cols = slice(g * GA * nh, (g + 1) * GA * nh)
            nc.scalar.activation(out=nrm[:, cols], in_=nrc[:, cols], func=ACT.Sqrt, bias=eps2[:])

        def chain_rec(g):
            cols = slice(g * GA * nh, (g + 1) * GA * nh)
            nc.vector.reciprocal(out=rinv[:, cols], in_=nrm[:, cols])

        def normalise(b, who):
            xw = xw_tiles[b]
            if b not in xn_tiles:
                xn = xnp.tile([P, nh, nf], BF16)
                xn_tiles[b] = xn
            xn = xn_tiles[b]
            for h in range(nh):
                j = b * nh + h
                if who == "S" and CS(b, h):
                    nc.scalar.activation(
                        out=xn[:, h, :], in_=xw[:, h, :], func=ACT.Copy, scale=rinv[:, j : j + 1]
                    )
                if who == "V" and CVV(b, h):
                    nc.vector.tensor_scalar(
                        out=xn[:, h, :], in0=xw[:, h, :], scalar1=rinv[:, j : j + 1],
                        scalar2=None, op0=ALU.mult,
                    )
                if who == "G" and not CS(b, h) and not CVV(b, h):
                    nc.gpsimd.tensor_scalar(
                        out=xn[:, h, :], in0=xw[:, h, :], scalar1=rinv[:, j : j + 1],
                        scalar2=0.0, op0=ALU.mult, op1=ALU.add,
                    )

        def transposes(b):
            xn = xn_tiles[b]
            words = xn[:].bitcast(F32)
            xt = pst.tile([P, nu, nn], F32)
            xt_tiles[b] = xt
            for h in range(nh):
                for u in range(nu):
                    nc.tensor.transpose(
                        xt[:, u, h * P : (h + 1) * P], words[:, h, u * P : (u + 1) * P], ident_w[:]
                    )

        def copy_out(b):
            xt = xt_tiles[b]
            grouped = grp.tile([P, nn, nt], BF16, align_bytes=64)
            gr_tiles[b] = grouped
            eng = nc.vector.tensor_copy if DV(b) else nc.scalar.copy
            eng(out=grouped[:].bitcast(F32), in_=xt[:].rearrange("p u r -> p r u"))

        mx_tiles = {}

        def quantise(b):
            grouped = gr_tiles[b]
            codes = mxp.tile([P, nn], U32, align_bytes=64)
            scl = mxp.tile([P, nn], U8, align_bytes=64)
            mx_tiles[b] = (codes, scl)
            nc.vector.quantize_mx(
                out=codes[:].bitcast(FP8X4), scales=scl[:],
                in_=grouped[:].rearrange("p r t -> p (r t)"),
            )

        acc_tiles = {}

        def mx(b):
            codes, scl = mx_tiles[b]
            acc = psa.tile([P, 3 * P], F32)
            acc_tiles[b] = acc
            nc.tensor.matmul_mx(
                out=acc[:, 0:P],
                lhsT=codes[:, P:nn].bitcast(FP8X4),
                lhsT_scale=scl[:, P:nn],
                rhs=codes[:, P:nn].bitcast(FP8X4),
                rhs_scale=scl[:, P:nn],
                start=True,
                stop=True,
            )
            nc.tensor.matmul_mx(
                out=acc[:, P : 3 * P],
                lhsT=codes[:, 0:P].bitcast(FP8X4),
                lhsT_scale=scl[:, 0:P],
                rhs=codes[:].bitcast(FP8X4),
                rhs_scale=scl[:],
                start=True,
                stop=True,
            )

        q_tiles = {}

        def parts(b):
            if TAIL and b == nb - 1:
                return [slice(2 * P, 3 * P), slice(0, 2 * P)]
            return [slice(0, 3 * P)]

        def mask(b):
            q = qp.tile([P, 3 * P], F32)
            q_tiles[b] = q
            for c in parts(b):
                nc.vector.tensor_scalar(
                    out=q[:, c], in0=acc_tiles[b][:, c], scalar1=EMP, scalar2=ZERO / EMP,
                    op0=ALU.is_gt, op1=ALU.max,
                )

        firsts = {}
        sizes = {}
        f = 0
        while f < nb:
            n = min(STORE_B, max(1, (nb - f) // 2))
            for i in range(n):
                firsts[f + i] = f
                sizes[f + i] = n
            f += n

        def first(b):
            return firsts[b]

        def size(b):
            return sizes[b]

        def last(b):
            return b == first(b) + size(b) - 1

        def apply(b):
            if b == first(b):
                o_new = op.tile([P, STORE_B, 4 * P], F32)
                o_tiles[b] = o_new
            o_sb = o_tiles[first(b)]
            i = b - first(b)
            if shared(b):
                scalar, op0, op1 = ZERO, ALU.max, ALU.min
            else:
                scalar, op0, op1 = EMP, ALU.max, ALU.mult
            for c in parts(b):
                nc.vector.scalar_tensor_tensor(
                    out=o_sb[:, i, P + c.start : P + c.stop], in0=acc_tiles[b][:, c], scalar=scalar,
                    in1=q_tiles[b][:, c], op0=op0, op1=op1,
                )
            if last(b):
                store(b, 0)

        r_tiles = {}

        def mirror(b):
            r = psb.tile([P, STORE_B, P], F32)
            r_tiles[b] = r
            for i in range(size(b)):
                nc.tensor.transpose(r[:, i, :], o_tiles[first(b)][:, i, 3 * P : 4 * P], ident_w[:])

        def mirror_out(b):
            n = size(b)
            if TV:
                nc.vector.tensor_copy(out=o_tiles[first(b)][:, 0:n, 0:P], in_=r_tiles[b][:, 0:n, :])
            else:
                nc.scalar.copy(out=o_tiles[first(b)][:, 0:n, 0:P], in_=r_tiles[b][:, 0:n, :])
            store(b, 1)

        def store(b, m):
            c0 = (1 - m) * nn
            f = first(b)
            nc.sync.dma_start(
                out=out[f : b + 1, m * P : (m + 1) * P, :].rearrange("b p j -> p b j"),
                in_=o_tiles[f][:, 0 : size(b), c0 : c0 + nn],
            )

        c_tiles = {}

        def rise(b):
            c = cp.tile([P, 3 * P], F32)
            c_tiles[b] = c
            nc.scalar.activation(
                out=c[:], in_=acc_tiles[b][:], func=ACT.Relu, scale=STEEP, bias=thr[:]
            )

        def floor_g(b):
            qg = cp.tile([P, 3 * P], F32)
            q_tiles[b] = qg
            nc.gpsimd.tensor_scalar(
                out=qg[:], in0=c_tiles[b][:], scalar1=1.0, scalar2=ZERO, op0=ALU.mult, op1=ALU.add
            )

        def floor_s(b):
            qs = cp.tile([P, 3 * P], F32)
            q_tiles[b] = qs
            nc.scalar.activation(
                out=qs[:], in_=c_tiles[b][:], func=ACT.Identity, bias=flo[:]
            )

        def on_g(b):
            return live(b) and MODG(b)

        def on_s(b):
            return live(b) and MODS(b)

        def shared(b):
            return on_g(b) or on_s(b)

        def live(b):
            return 0 <= b < nb

        def group_end(e):
            return live(e) and e % GA == GA - 1

        def store_end(e):
            return live(e) and last(e)

        for b in AG:
            mul_w(b)
        for s in range(nb + D_L + 1):
            if live(s - D_M):
                mx(s - D_M)
            if live(s - D_T):
                transposes(s - D_T)
            if store_end(s - D_R):
                mirror(s - D_R)
            if live(s - D_H) and not shared(s - D_H):
                mask(s - D_H)
            if live(s) and s not in AG:
                mul_w(s)
            if live(s - D_S):
                sumsq_v(s - D_S)
            if not live(s) and live(s - D_Q):
                quantise(s - D_Q)
            if live(s - D_A):
                apply(s - D_A)
            if live(s - D_N):
                normalise(s - D_N, "V")
            if group_end(s - D_CH) and REC_FIRST:
                chain_rec((s - D_CH) // GA)
            if live(s) and live(s - D_Q):
                quantise(s - D_Q)
            if group_end(s - D_CH) and not REC_FIRST:
                chain_rec((s - D_CH) // GA)
            if live(s - D_C) and DV(s - D_C):
                copy_out(s - D_C)
            for k in ORDER_S:
                if k == "B" and live(s - D_S):
                    sumsq(s - D_S)
                if k == "b" and live(s - D_S):
                    sumsq(s - D_S, (0,))
                if k == "c" and live(s - D_S):
                    sumsq(s - D_S, (1,))
                if k == "l" and group_end(s - D_S):
                    chain_relu((s - D_S) // GA)
                if k == "q" and group_end(s - D_S):
                    chain_sqrt((s - D_S) // GA)
                if k == "L" and group_end(s - D_S - 1):
                    chain_relu((s - D_S - 1) // GA)
                if k == "Q" and group_end(s - D_S - 1):
                    chain_sqrt((s - D_S - 1) // GA)
                if k == "N" and live(s - D_N):
                    normalise(s - D_N, "S")
                if k == "D" and live(s - D_C) and not DV(s - D_C):
                    copy_out(s - D_C)
                if k == "r" and shared(s - D_F):
                    rise(s - D_F)
                if k == "f" and on_s(s - D_G):
                    floor_s(s - D_G)
                if k == "m" and store_end(s - D_L):
                    mirror_out(s - D_L)
            if live(s - D_N):
                normalise(s - D_N, "G")
            if on_g(s - D_G):
                floor_g(s - D_G)
